import numpy as np
import ml_dtypes


def mxq(x, axis, fmt="e4m3"):
    dtype, down = {"e4m3": (ml_dtypes.float8_e4m3fn, 7), "e5m2": (ml_dtypes.float8_e5m2, 14)}[fmt]
    v = np.moveaxis(np.asarray(x, np.float32).astype(ml_dtypes.bfloat16).astype(np.float64), axis, -1)
    blocks = v.reshape(v.shape[:-1] + (-1, 32))
    amax = np.abs(blocks).max(-1, keepdims=True)
    byte = np.maximum(np.where(amax > 0, np.frexp(amax)[1] - 1 + 127, 0) - down, 1)
    scale = np.exp2(byte - 127.0)
    codes = (blocks / scale).astype(np.float32).astype(dtype).astype(np.float64)
    return np.moveaxis((codes * scale).reshape(v.shape), -1, axis)


WIDE = False


def mx_kscale(k):
    if not WIDE:
        return np.ones(k)
    levels = np.array([10, -10, 5, -5, 0])
    if k % 512:
        return np.exp2(np.random.permutation(np.resize(levels, k // 32))).repeat(32)
    a = np.empty((k // 512, 16))
    for p in range(k // 512):
        a[p, :8] = np.random.permutation(np.resize(levels, 8))
        for g in range(8):
            far = levels[np.abs(levels - a[p, g]) >= 10]
            a[p, g + 8] = far[np.random.randint(len(far))]
    return np.exp2(a.ravel()).repeat(32)


BF16 = ml_dtypes.bfloat16


def bf(x):
    return np.asarray(x, np.float32).astype(BF16)


def f64(x):
    return np.asarray(x).astype(np.float64)


B, SEQ, DIM, N_HEADS, N_KV, HEAD, HIDDEN = 1, 512, 2048, 16, 4, 128, 5504
ROPE_THETA = 10000.0
HALF = HEAD // 2


def rope(t, cos, sin):
    t2 = t.reshape(*t.shape[:-1], HALF, 2)
    t0, t1 = t2[..., 0], t2[..., 1]
    c = cos[None, :, None, :]
    s = sin[None, :, None, :]
    out = np.stack([t0 * c - t1 * s, t0 * s + t1 * c], axis=-1)
    return out.reshape(t.shape)


def draw0():
    s = mx_kscale(DIM)
    inv = 1.0 / (ROPE_THETA ** (np.arange(0, HEAD, 2) / HEAD))
    freqs = np.outer(np.arange(SEQ), inv)
    return {"x": bf(np.random.standard_normal((B, SEQ, DIM)) * s),
            "freqs_cos": bf(np.cos(freqs)),
            "freqs_sin": bf(np.sin(freqs)),
            "wq": bf(np.random.standard_normal((DIM, N_HEADS * HEAD)) * 1.25 / np.sqrt(DIM) / s[:, None]),
            "wk": bf(np.random.standard_normal((DIM, N_KV * HEAD)) * 1.25 / np.sqrt(DIM) / s[:, None]),
            "wv": bf(np.random.standard_normal((DIM, N_KV * HEAD)) * 1.5 / np.sqrt(DIM) / s[:, None])}


def core(x, freqs_cos, freqs_sin, wq, wk, wv):
    xm = mxq(f64(x).reshape(B * SEQ, DIM), 1, "e4m3")
    q = (xm @ mxq(f64(wq), 0, "e4m3")).reshape(B, SEQ, N_HEADS, HEAD)
    k = (xm @ mxq(f64(wk), 0, "e4m3")).reshape(B, SEQ, N_KV, HEAD)
    v = (xm @ mxq(f64(wv), 0, "e4m3")).reshape(B, SEQ, N_KV, HEAD)
    c, s = f64(freqs_cos), f64(freqs_sin)
    return rope(q, c, s), rope(k, c, s), v


def e4m3fn_bytes(y):
    return np.clip(np.asarray(y, np.float64), -448.0, 448.0).astype(np.float32).astype(ml_dtypes.float8_e4m3fn).view(np.uint8)


def e4m3fn_values(b):
    return np.asarray(b, np.uint8).view(ml_dtypes.float8_e4m3fn).astype(np.float64)


def setup_inputs():
    d = draw0()
    x0 = np.asarray(d['wq']).astype(np.float64)
    s = (np.max(np.abs(x0), axis=(1,), keepdims=True) / 448.0).astype(np.float32)
    out = {}
    for k, v in d.items():
        if k == 'wq':
            out['wq_bytes'] = e4m3fn_bytes(x0 / s.astype(np.float64))
            out['wq_scale'] = s
        else:
            out[k] = v
    return out


def reference(x, freqs_cos, freqs_sin, wq_bytes, wq_scale, wk, wv):
    return core(x, freqs_cos, freqs_sin, e4m3fn_values(wq_bytes) * wq_scale.astype(np.float64), wk, wv)

@@ -1,0 +1,270 @@
+from contextlib import ExitStack
+
+import concourse.mybir as mybir
+from concourse.masks import make_identity
+
+SEQ, DIM, HEAD = 512, 2048, 128
+N_Q, N_K, N_V = 2048, 512, 512
+FLOPS = 2 * SEQ * DIM * (N_Q + N_K + N_V)
+
+F32 = mybir.dt.float32
+BF16 = mybir.dt.bfloat16
+U32 = mybir.dt.uint32
+U8 = mybir.dt.uint8
+E4M3 = mybir.dt.float8_e4m3fn
+FP8X4 = mybir.dt.float8_e4m3fn_x4
+MULT = mybir.AluOpType.mult
+ADD = mybir.AluOpType.add
+COPY = mybir.ActivationFunctionType.Copy
+
+P = 128
+PACK = 4
+PASSES = DIM // (P * PACK)
+TOK_TILES = SEQ // P
+CHUNK = 512
+HEADS_PER_CHUNK = CHUNK // HEAD
+Q_CHUNKS = N_Q // CHUNK
+CHUNKS = Q_CHUNKS + 2
+UNITS = CHUNKS * PASSES
+ROPED = (CHUNKS - 1) * TOK_TILES
+
+HEAD_UNITS = 9
+UNITS_BEFORE_X = 10
+FIRST_SCALAR_UNIT = 15
+WIDEN_AHEAD = 6
+ROPE_AFTER = {9: (0, 1), 13: (2,), 17: (3,), 21: (4,)}
+VECTOR_ADDS = 2
+
+
+def tile_transformerblock_pa_kernel(
+    tc, x, freqs_cos, freqs_sin, wq_bytes, wq_scale, wk, wv, out_0, out_1, out_2
+):
+    nc = tc.nc
+    x_rows = x.rearrange("b s d -> (b s) d")
+    wq_view = wq_bytes.rearrange("(g p t) n -> g p t n", p=P, t=PACK)
+    wk_view = wk.rearrange("(g p t) n -> g p t n", p=P, t=PACK)
+    wv_view = wv.rearrange("(g p t) n -> g p t n", p=P, t=PACK)
+    q_out = out_0.rearrange("b s h d -> (b s) (h d)")
+    k_out = out_1.rearrange("b s h d -> (b s) (h d)")
+    v_out = out_2.rearrange("b s h d -> (b s) (h d)")
+
+    with ExitStack() as ctx:
+        keep = ctx.enter_context(tc.tile_pool(name="keep", bufs=1))
+        planes = ctx.enter_context(tc.tile_pool(name="planes", bufs=7))
+        grouped = ctx.enter_context(tc.tile_pool(name="grouped", bufs=4))
+        quant = ctx.enter_context(tc.tile_pool(name="quant", bufs=12))
+        rope = ctx.enter_context(tc.tile_pool(name="rope", bufs=4))
+        result = ctx.enter_context(tc.tile_pool(name="result", bufs=6))
+        psum = ctx.enter_context(tc.psum_pool(name="psum", bufs=8))
+        ctx.enter_context(tc.manual_schedule())
+
+        scales = keep.tile([P, PASSES, PACK], F32, name="scales")
+        wq_codes = [keep.tile([P, PASSES * PACK, CHUNK], U8, name="wq_codes%d" % j) for j in range(Q_CHUNKS)]
+        x_raw = [keep.tile([P, DIM], BF16, name="x_raw%d" % m) for m in range(TOK_TILES)]
+        wk_raw = keep.tile([P, PASSES * PACK, CHUNK], BF16, name="wk_raw")
+        wv_raw = keep.tile([P, PASSES * PACK, CHUNK], BF16, name="wv_raw")
+        cos_raw = keep.tile([P, TOK_TILES, HEAD // 2], BF16, name="cos_raw")
+        sin_raw = keep.tile([P, TOK_TILES, HEAD // 2], BF16, name="sin_raw")
+
+        def load_wq(j, g):
+            nc.sync.dma_start(
+                out=wq_codes[j][:, PACK * g : PACK * (g + 1), :],
+                in_=wq_view[g][:, :, CHUNK * j : CHUNK * (j + 1)],
+            )
+
+        nc.sync.dma_start(
+            out=scales[:], in_=wq_scale.rearrange("(g p t) o -> p g (t o)", p=P, t=PACK)
+        )
+        for g in range(PASSES):
+            load_wq(0, g)
+            nc.sync.dma_start(out=wk_raw[:, PACK * g : PACK * (g + 1), :], in_=wk_view[g])
+        for u in range(2 * PASSES, UNITS_BEFORE_X):
+            load_wq(u // PASSES - 1, u % PASSES)
+        for m in range(TOK_TILES):
+            nc.sync.dma_start(out=x_raw[m][:], in_=x_rows[P * m : P * (m + 1), :])
+        nc.sync.dma_start(out=cos_raw[:], in_=freqs_cos.rearrange("(m p) i -> p m i", p=P))
+        nc.sync.dma_start(out=sin_raw[:], in_=freqs_sin.rearrange("(m p) i -> p m i", p=P))
+        for u in range(UNITS_BEFORE_X, PASSES * (Q_CHUNKS + 1)):
+            load_wq(u // PASSES - 1, u % PASSES)
+        for g in range(PASSES):
+            nc.sync.dma_start(out=wv_raw[:, PACK * g : PACK * (g + 1), :], in_=wv_view[g])
+
+        zero = keep.tile([P, 1], F32, name="zero")
+        warm = keep.tile([P, 1], F32, name="warm")
+        nc.vector.memset(zero[:], 0.0)
+        nc.scalar.activation(out=warm[:], in_=zero[:], func=COPY)
+        ident = keep.tile([P, P], F32, name="ident")
+        make_identity(nc, ident[:])
+
+        cos_tab = keep.tile([P, TOK_TILES, HEAD], F32, name="cos_tab")
+        sin_tab = keep.tile([P, TOK_TILES, HEAD], F32, name="sin_tab")
+        cos_pairs = cos_tab[:].rearrange("p m (i e) -> p m i e", e=2)
+        sin_pairs = sin_tab[:].rearrange("p m (i e) -> p m i e", e=2)
+        nc.gpsimd.tensor_copy(out=cos_pairs[:, :, :, 0], in_=cos_raw[:])
+        nc.gpsimd.tensor_copy(out=cos_pairs[:, :, :, 1], in_=cos_raw[:])
+        nc.gpsimd.tensor_copy(out=sin_pairs[:, :, :, 1], in_=sin_raw[:])
+        nc.gpsimd.tensor_scalar(
+            out=sin_pairs[:, :, :, 0], in0=sin_raw[:], scalar1=-1.0, scalar2=0.0, op0=MULT, op1=ADD
+        )
+
+        x_codes = [keep.tile([P, PASSES * P], U32, name="x_codes%d" % m, align_bytes=64) for m in range(TOK_TILES)]
+        x_scales = [keep.tile([P, PASSES * P], U8, name="x_scales%d" % m, align_bytes=64) for m in range(TOK_TILES)]
+        x_grouped = {}
+
+        def turn_x(m):
+            words = x_raw[m][:].bitcast(F32)
+            x_grouped[m] = grouped.tile([P, PASSES * P * PACK], BF16, name="x_grouped", align_bytes=64)
+            x_words = x_grouped[m][:].bitcast(F32).rearrange("p (g r u) -> p g r u", g=PASSES, u=2)
+            for half in range(2):
+                turned = psum.tile([P, 2, 2, P], F32, name="turned", tag="bank")
+                for gg in range(2):
+                    g = 2 * half + gg
+                    for u in range(2):
+                        nc.tensor.transpose(
+                            turned[:, gg, u, :], words[:, 256 * g + u : 256 * (g + 1) : 2], ident[:]
+                        )
+                nc.scalar.copy(
+                    out=x_words[:, 2 * half : 2 * half + 2, :, :],
+                    in_=turned[:].rearrange("p g u r -> p g r u"),
+                )
+
+        def quantise_x(m):
+            nc.vector.quantize_mx(
+                out=x_codes[m][:].bitcast(FP8X4), scales=x_scales[m][:], in_=x_grouped[m][:]
+            )
+
+        wide = {}
+        packed = {}
+        w_codes = {}
+        w_scales = {}
+        acc = {}
+        by_cos = {}
+        by_sin = {}
+
+        def widen(u):
+            c, g = divmod(u, PASSES)
+            wide[u] = planes.tile([P, PACK, CHUNK], BF16, name="wide")
+            for t in range(PACK):
+                nc.scalar.activation(
+                    out=wide[u][:, t, :],
+                    in_=wq_codes[c - 1][:, PACK * g + t, :].bitcast(E4M3),
+                    func=COPY,
+                    scale=scales[:, g, t : t + 1],
+                )
+
+        def interleave(u):
+            c, g = divmod(u, PASSES)
+            if c == 0:
+                rows = wk_raw[:, PACK * g : PACK * (g + 1), :]
+            elif c == CHUNKS - 1:
+                rows = wv_raw[:, PACK * g : PACK * (g + 1), :]
+            else:
+                rows = wide[u][:]
+            packed[u] = grouped.tile([P, CHUNK * PACK], BF16, name="packed", align_bytes=64)
+            dst = packed[u][:].rearrange("p (c i t) -> p c t i", i=4, t=PACK)
+            src = rows.rearrange("p t (c i) -> p c t i", i=4)
+            if u >= FIRST_SCALAR_UNIT:
+                nc.scalar.copy(out=dst, in_=src)
+            else:
+                nc.vector.tensor_copy(out=dst, in_=src)
+
+        def quantise(u):
+            w_codes[u] = quant.tile([P, CHUNK], U32, name="w_codes", align_bytes=64)
+            w_scales[u] = quant.tile([P, CHUNK], U8, name="w_scales", align_bytes=64)
+            nc.vector.quantize_mx(
+                out=w_codes[u][:].bitcast(FP8X4), scales=w_scales[u][:], in_=packed[u][:]
+            )
+
+        def multiply(c, m, g):
+            if g == 0:
+                acc[(c, m)] = psum.tile([P, CHUNK], F32, name="acc", tag="bank")
+            u = PASSES * c + g
+            cols = slice(P * g, P * (g + 1))
+            nc.tensor.matmul_mx(
+                out=acc[(c, m)][:],
+                lhsT=x_codes[m][:, cols].bitcast(FP8X4),
+                lhsT_scale=x_scales[m][:, cols],
+                rhs=w_codes[u][:].bitcast(FP8X4),
+                rhs_scale=w_scales[u][:],
+                start=(g == 0),
+                stop=(g == PASSES - 1),
+            )
+
+        def times_tables(b):
+            c, m = divmod(b, TOK_TILES)
+            by_cos[b] = rope.tile([P, CHUNK], F32, name="by_cos")
+            by_sin[b] = rope.tile([P, CHUNK], F32, name="by_sin")
+            nc.vector.tensor_tensor(
+                out=by_cos[b][:].rearrange("p (h d) -> p h d", d=HEAD),
+                in0=acc[(c, m)][:].rearrange("p (h d) -> p h d", d=HEAD),
+                in1=cos_tab[:, m : m + 1, :].to_broadcast([P, HEADS_PER_CHUNK, HEAD]),
+                op=MULT,
+            )
+            nc.vector.tensor_tensor(
+                out=by_sin[b][:].rearrange("p (h i e) -> p h i e", h=HEADS_PER_CHUNK, e=2),
+                in0=acc[(c, m)][:].rearrange("p (h i e) -> p h i e", h=HEADS_PER_CHUNK, e=2)[:, :, :, ::-1],
+                in1=sin_tab[:, m : m + 1, :]
+                .rearrange("p o (i e) -> p o i e", e=2)
+                .to_broadcast([P, HEADS_PER_CHUNK, HEAD // 2, 2]),
+                op=MULT,
+            )
+
+        def add_and_store(b, engine):
+            c, m = divmod(b, TOK_TILES)
+            res = result.tile([P, CHUNK], F32, name="res")
+            engine.tensor_tensor(out=res[:], in0=by_cos[b][:], in1=by_sin[b][:], op=ADD)
+            rows = slice(P * m, P * (m + 1))
+            if c == 0:
+                nc.sync.dma_start(out=k_out[rows, :], in_=res[:])
+            else:
+                nc.sync.dma_start(out=q_out[rows, CHUNK * (c - 1) : CHUNK * c], in_=res[:])
+
+        def copy_and_store(m):
+            res = result.tile([P, CHUNK], F32, name="res")
+            if m % 2 == 0:
+                nc.scalar.copy(out=res[:], in_=acc[(CHUNKS - 1, m)][:])
+            else:
+                nc.vector.tensor_copy(out=res[:], in_=acc[(CHUNKS - 1, m)][:])
+            nc.sync.dma_start(out=v_out[P * m : P * (m + 1), :], in_=res[:])
+
+        first_q, last_q = PASSES, PASSES * (Q_CHUNKS + 1)
+        for u in range(first_q, UNITS_BEFORE_X):
+            widen(u)
+        for m in range(TOK_TILES):
+            turn_x(m)
+        widened = UNITS_BEFORE_X
+        passes_issued = 2 * PASSES
+        left_to_vector = []
+        interleave(0)
+        for u in range(UNITS):
+            while widened < min(u + WIDEN_AHEAD, last_q):
+                widen(widened)
+                widened += 1
+            if u == HEAD_UNITS:
+                for m in range(TOK_TILES):
+                    quantise_x(m)
+            if u + 1 < UNITS:
+                interleave(u + 1)
+            quantise(u)
+            if u < HEAD_UNITS:
+                continue
+            if u <= UNITS - PASSES or u == UNITS - 1:
+                for b in left_to_vector:
+                    add_and_store(b, nc.vector)
+                left_to_vector = []
+            if u == HEAD_UNITS:
+                for b in range(2 * TOK_TILES):
+                    for g in range(PASSES):
+                        multiply(b // TOK_TILES, b % TOK_TILES, g)
+            group = [TOK_TILES * c + m for c in ROPE_AFTER.get(u, ()) for m in range(TOK_TILES)]
+            for i, b in enumerate(group):
+                times_tables(b)
+                if 0 < i <= len(group) - VECTOR_ADDS:
+                    add_and_store(b - 1, nc.gpsimd)
+            left_to_vector = left_to_vector + group[len(group) - VECTOR_ADDS :]
+            while passes_issued <= u:
+                for m in range(TOK_TILES):
+                    multiply(passes_issued // PASSES, m, passes_issued % PASSES)
+                passes_issued += 1
+        for m in range(TOK_TILES):
+            copy_and_store(m)

@@ -72,6 +72,8 @@ def tile_transformerblock_pa_kernel(
                 in_=wq_view[g][:, :, CHUNK * j : CHUNK * (j + 1)],
             )
 
+        nc.sync.dma_start(out=cos_raw[:], in_=freqs_cos.rearrange("(m p) i -> p m i", p=P))
+        nc.sync.dma_start(out=sin_raw[:], in_=freqs_sin.rearrange("(m p) i -> p m i", p=P))
         nc.sync.dma_start(
             out=scales[:], in_=wq_scale.rearrange("(g p t) o -> p g (t o)", p=P, t=PACK)
         )
@@ -82,8 +84,6 @@ def tile_transformerblock_pa_kernel(
             load_wq(u // PASSES - 1, u % PASSES)
         for m in range(TOK_TILES):
             nc.sync.dma_start(out=x_raw[m][:], in_=x_rows[P * m : P * (m + 1), :])
-        nc.sync.dma_start(out=cos_raw[:], in_=freqs_cos.rearrange("(m p) i -> p m i", p=P))
-        nc.sync.dma_start(out=sin_raw[:], in_=freqs_sin.rearrange("(m p) i -> p m i", p=P))
         for u in range(UNITS_BEFORE_X, PASSES * (Q_CHUNKS + 1)):
             load_wq(u // PASSES - 1, u % PASSES)
         for g in range(PASSES):
@@ -98,13 +98,19 @@ def tile_transformerblock_pa_kernel(
 
         cos_tab = keep.tile([P, TOK_TILES, HEAD], F32, name="cos_tab")
         sin_tab = keep.tile([P, TOK_TILES, HEAD], F32, name="sin_tab")
-        cos_pairs = cos_tab[:].rearrange("p m (i e) -> p m i e", e=2)
-        sin_pairs = sin_tab[:].rearrange("p m (i e) -> p m i e", e=2)
-        nc.gpsimd.tensor_copy(out=cos_pairs[:, :, :, 0], in_=cos_raw[:])
-        nc.gpsimd.tensor_copy(out=cos_pairs[:, :, :, 1], in_=cos_raw[:])
-        nc.gpsimd.tensor_copy(out=sin_pairs[:, :, :, 1], in_=sin_raw[:])
-        nc.gpsimd.tensor_scalar(
-            out=sin_pairs[:, :, :, 0], in0=sin_raw[:], scalar1=-1.0, scalar2=0.0, op0=MULT, op1=ADD
+        sign = keep.tile([P, 2], F32, name="sign")
+        nc.vector.memset(sign[:, 0:1], -1.0)
+        nc.vector.memset(sign[:, 1:2], 1.0)
+        pairs = [P, TOK_TILES * HEAD // 2, 2]
+        nc.vector.tensor_copy(
+            out=cos_tab[:].rearrange("p m (i e) -> p (m i) e", e=2),
+            in_=cos_raw[:].rearrange("p m i -> p (m i)").unsqueeze(2).to_broadcast(pairs),
+        )
+        nc.vector.tensor_tensor(
+            out=sin_tab[:].rearrange("p m (i e) -> p (m i) e", e=2),
+            in0=sin_raw[:].rearrange("p m i -> p (m i)").unsqueeze(2).to_broadcast(pairs),
+            in1=sign[:].unsqueeze(1).to_broadcast(pairs),
+            op=MULT,
         )
 
         x_codes = [keep.tile([P, PASSES * P], U32, name="x_codes%d" % m, align_bytes=64) for m in range(TOK_TILES)]

@@ -86,8 +86,6 @@ def tile_transformerblock_pa_kernel(
             nc.sync.dma_start(out=x_raw[m][:], in_=x_rows[P * m : P * (m + 1), :])
         for u in range(UNITS_BEFORE_X, PASSES * (Q_CHUNKS + 1)):
             load_wq(u // PASSES - 1, u % PASSES)
-        for g in range(PASSES):
-            nc.sync.dma_start(out=wv_raw[:, PACK * g : PACK * (g + 1), :], in_=wv_view[g])
 
         zero = keep.tile([P, 1], F32, name="zero")
         warm = keep.tile([P, 1], F32, name="warm")
@@ -241,7 +239,11 @@ def tile_transformerblock_pa_kernel(
         widened = UNITS_BEFORE_X
         passes_issued = 2 * PASSES
         left_to_vector = []
-        interleave(0)
+
+        def unit_at(i):
+            return (i % 2) * PASSES + i // 2 if i < 2 * PASSES else i
+
+        interleave(unit_at(0))
         for u in range(UNITS):
             while widened < min(u + WIDEN_AHEAD, last_q):
                 widen(widened)
@@ -250,8 +252,8 @@ def tile_transformerblock_pa_kernel(
                 for m in range(TOK_TILES):
                     quantise_x(m)
             if u + 1 < UNITS:
-                interleave(u + 1)
-            quantise(u)
+                interleave(unit_at(u + 1))
+            quantise(unit_at(u))
             if u < HEAD_UNITS:
                 continue
             if u <= UNITS - PASSES or u == UNITS - 1:
@@ -268,6 +270,9 @@ def tile_transformerblock_pa_kernel(
                 if 0 < i <= len(group) - VECTOR_ADDS:
                     add_and_store(b - 1, nc.gpsimd)
             left_to_vector = left_to_vector + group[len(group) - VECTOR_ADDS :]
+            if u == HEAD_UNITS:
+                for g in range(PASSES):
+                    nc.sync.dma_start(out=wv_raw[:, PACK * g : PACK * (g + 1), :], in_=wv_view[g])
             while passes_issued <= u:
                 for m in range(TOK_TILES):
                     multiply(passes_issued // PASSES, m, passes_issued % PASSES)

@@ -34,6 +34,7 @@ FIRST_SCALAR_UNIT = 15
 WIDEN_AHEAD = 6
 ROPE_AFTER = {9: (0, 1), 13: (2,), 17: (3,), 21: (4,)}
 VECTOR_ADDS = 2
+RUN = 8
 
 
 def tile_transformerblock_pa_kernel(
@@ -94,20 +95,19 @@ def tile_transformerblock_pa_kernel(
         ident = keep.tile([P, P], F32, name="ident")
         make_identity(nc, ident[:])
 
-        cos_tab = keep.tile([P, TOK_TILES, HEAD], F32, name="cos_tab")
-        sin_tab = keep.tile([P, TOK_TILES, HEAD], F32, name="sin_tab")
+        tables = keep.tile([P, TOK_TILES, 2, HEAD], F32, name="tables")
         sign = keep.tile([P, 2], F32, name="sign")
-        nc.vector.memset(sign[:, 0:1], -1.0)
-        nc.vector.memset(sign[:, 1:2], 1.0)
-        pairs = [P, TOK_TILES * HEAD // 2, 2]
+        nc.vector.memset(sign[:, 0:1], 1.0)
+        nc.vector.memset(sign[:, 1:2], -1.0)
+        pairs = [P, TOK_TILES, HEAD // 2, 2]
         nc.vector.tensor_copy(
-            out=cos_tab[:].rearrange("p m (i e) -> p (m i) e", e=2),
-            in_=cos_raw[:].rearrange("p m i -> p (m i)").unsqueeze(2).to_broadcast(pairs),
+            out=tables[:, :, 0, :].rearrange("p m (i e) -> p m i e", e=2),
+            in_=cos_raw[:].unsqueeze(3).to_broadcast(pairs),
         )
         nc.vector.tensor_tensor(
-            out=sin_tab[:].rearrange("p m (i e) -> p (m i) e", e=2),
-            in0=sin_raw[:].rearrange("p m i -> p (m i)").unsqueeze(2).to_broadcast(pairs),
-            in1=sign[:].unsqueeze(1).to_broadcast(pairs),
+            out=tables[:, :, 1, :].rearrange("p m (i e) -> p m i e", e=2),
+            in0=sin_raw[:].unsqueeze(3).to_broadcast(pairs),
+            in1=sign[:].unsqueeze(1).unsqueeze(1).to_broadcast(pairs),
             op=MULT,
         )
 
@@ -142,8 +142,7 @@ def tile_transformerblock_pa_kernel(
         w_codes = {}
         w_scales = {}
         acc = {}
-        by_cos = {}
-        by_sin = {}
+        both = {}
 
         def widen(u):
             c, g = divmod(u, PASSES)
@@ -165,8 +164,8 @@ def tile_transformerblock_pa_kernel(
             else:
                 rows = wide[u][:]
             packed[u] = grouped.tile([P, CHUNK * PACK], BF16, name="packed", align_bytes=64)
-            dst = packed[u][:].rearrange("p (c i t) -> p c t i", i=4, t=PACK)
-            src = rows.rearrange("p t (c i) -> p c t i", i=4)
+            dst = packed[u][:].rearrange("p (c i t) -> p c t i", i=RUN, t=PACK)
+            src = rows.rearrange("p t (c i) -> p c t i", i=RUN)
             if u >= FIRST_SCALAR_UNIT:
                 nc.scalar.copy(out=dst, in_=src)
             else:
@@ -196,27 +195,24 @@ def tile_transformerblock_pa_kernel(
 
         def times_tables(b):
             c, m = divmod(b, TOK_TILES)
-            by_cos[b] = rope.tile([P, CHUNK], F32, name="by_cos")
-            by_sin[b] = rope.tile([P, CHUNK], F32, name="by_sin")
+            both[b] = rope.tile([P, 2, CHUNK], F32, name="both")
+            shape = [P, 2, HEADS_PER_CHUNK, HEAD]
             nc.vector.tensor_tensor(
-                out=by_cos[b][:].rearrange("p (h d) -> p h d", d=HEAD),
-                in0=acc[(c, m)][:].rearrange("p (h d) -> p h d", d=HEAD),
-                in1=cos_tab[:, m : m + 1, :].to_broadcast([P, HEADS_PER_CHUNK, HEAD]),
-                op=MULT,
-            )
-            nc.vector.tensor_tensor(
-                out=by_sin[b][:].rearrange("p (h i e) -> p h i e", h=HEADS_PER_CHUNK, e=2),
-                in0=acc[(c, m)][:].rearrange("p (h i e) -> p h i e", h=HEADS_PER_CHUNK, e=2)[:, :, :, ::-1],
-                in1=sin_tab[:, m : m + 1, :]
-                .rearrange("p o (i e) -> p o i e", e=2)
-                .to_broadcast([P, HEADS_PER_CHUNK, HEAD // 2, 2]),
+                out=both[b][:].rearrange("p s (h d) -> p s h d", d=HEAD),
+                in0=acc[(c, m)][:].rearrange("p (h d) -> p h d", d=HEAD).unsqueeze(1).to_broadcast(shape),
+                in1=tables[:, m, :, :].unsqueeze(2).to_broadcast(shape),
                 op=MULT,
             )
 
         def add_and_store(b, engine):
             c, m = divmod(b, TOK_TILES)
             res = result.tile([P, CHUNK], F32, name="res")
-            engine.tensor_tensor(out=res[:], in0=by_cos[b][:], in1=by_sin[b][:], op=ADD)
+            engine.tensor_tensor(
+                out=res[:].rearrange("p (j e) -> p j e", e=2),
+                in0=both[b][:, 0, :].rearrange("p (j e) -> p j e", e=2),
+                in1=both[b][:, 1, :].rearrange("p (j e) -> p j e", e=2)[:, :, ::-1],
+                op=ADD,
+            )
             rows = slice(P * m, P * (m + 1))
             if c == 0:
                 nc.sync.dma_start(out=k_out[rows, :], in_=res[:])

@@ -15,6 +15,7 @@ E4M3 = mybir.dt.float8_e4m3fn
 FP8X4 = mybir.dt.float8_e4m3fn_x4
 MULT = mybir.AluOpType.mult
 ADD = mybir.AluOpType.add
+SUB = mybir.AluOpType.subtract
 COPY = mybir.ActivationFunctionType.Copy
 
 P = 128
@@ -26,15 +27,17 @@ HEADS_PER_CHUNK = CHUNK // HEAD
 Q_CHUNKS = N_Q // CHUNK
 CHUNKS = Q_CHUNKS + 2
 UNITS = CHUNKS * PASSES
-ROPED = (CHUNKS - 1) * TOK_TILES
+HALF = CHUNK // 2
 
-HEAD_UNITS = 9
+THREE_PRODUCTS = (1, 3)
+HEAD_UNITS = 7
 UNITS_BEFORE_X = 10
-FIRST_SCALAR_UNIT = 15
+FIRST_SCALAR_UNIT = 16
 WIDEN_AHEAD = 6
-ROPE_AFTER = {9: (0, 1), 13: (2,), 17: (3,), 21: (4,)}
+ROPE_AFTER = {9: (0,), 12: (1,), 15: (2,), 19: (3,), 22: (4,)}
 VECTOR_ADDS = 2
 RUN = 8
+PSUM_BANKS = 8
 
 
 def tile_transformerblock_pa_kernel(
@@ -55,8 +58,8 @@ def tile_transformerblock_pa_kernel(
         grouped = ctx.enter_context(tc.tile_pool(name="grouped", bufs=4))
         quant = ctx.enter_context(tc.tile_pool(name="quant", bufs=12))
         rope = ctx.enter_context(tc.tile_pool(name="rope", bufs=4))
-        result = ctx.enter_context(tc.tile_pool(name="result", bufs=6))
-        psum = ctx.enter_context(tc.psum_pool(name="psum", bufs=8))
+        result = ctx.enter_context(tc.tile_pool(name="result", bufs=8))
+        psum = ctx.enter_context(tc.psum_pool(name="psum", bufs=PSUM_BANKS))
         ctx.enter_context(tc.manual_schedule())
 
         scales = keep.tile([P, PASSES, PACK], F32, name="scales")
@@ -73,13 +76,14 @@ def tile_transformerblock_pa_kernel(
                 in_=wq_view[g][:, :, CHUNK * j : CHUNK * (j + 1)],
             )
 
-        nc.sync.dma_start(out=cos_raw[:], in_=freqs_cos.rearrange("(m p) i -> p m i", p=P))
-        nc.sync.dma_start(out=sin_raw[:], in_=freqs_sin.rearrange("(m p) i -> p m i", p=P))
         nc.sync.dma_start(
             out=scales[:], in_=wq_scale.rearrange("(g p t) o -> p g (t o)", p=P, t=PACK)
         )
         for g in range(PASSES):
             load_wq(0, g)
+            if g == 0:
+                nc.sync.dma_start(out=cos_raw[:], in_=freqs_cos.rearrange("(m p) i -> p m i", p=P))
+                nc.sync.dma_start(out=sin_raw[:], in_=freqs_sin.rearrange("(m p) i -> p m i", p=P))
             nc.sync.dma_start(out=wk_raw[:, PACK * g : PACK * (g + 1), :], in_=wk_view[g])
         for u in range(2 * PASSES, UNITS_BEFORE_X):
             load_wq(u // PASSES - 1, u % PASSES)
@@ -95,20 +99,20 @@ def tile_transformerblock_pa_kernel(
         ident = keep.tile([P, P], F32, name="ident")
         make_identity(nc, ident[:])
 
-        tables = keep.tile([P, TOK_TILES, 2, HEAD], F32, name="tables")
         sign = keep.tile([P, 2], F32, name="sign")
         nc.vector.memset(sign[:, 0:1], 1.0)
         nc.vector.memset(sign[:, 1:2], -1.0)
-        pairs = [P, TOK_TILES, HEAD // 2, 2]
-        nc.vector.tensor_copy(
-            out=tables[:, :, 0, :].rearrange("p m (i e) -> p m i e", e=2),
-            in_=cos_raw[:].unsqueeze(3).to_broadcast(pairs),
+        signed_sin = keep.tile([P, TOK_TILES, HEAD // 2, 2], F32, name="signed_sin")
+        turn = keep.tile([P, TOK_TILES, HEAD // 2, 2], F32, name="turn")
+        table = [P, TOK_TILES, HEAD // 2, 2]
+        nc.vector.tensor_tensor(
+            out=signed_sin[:],
+            in0=sin_raw[:].unsqueeze(3).to_broadcast(table),
+            in1=sign[:].unsqueeze(1).unsqueeze(1).to_broadcast(table),
+            op=MULT,
         )
         nc.vector.tensor_tensor(
-            out=tables[:, :, 1, :].rearrange("p m (i e) -> p m i e", e=2),
-            in0=sin_raw[:].unsqueeze(3).to_broadcast(pairs),
-            in1=sign[:].unsqueeze(1).unsqueeze(1).to_broadcast(pairs),
-            op=MULT,
+            out=turn[:], in0=signed_sin[:], in1=cos_raw[:].unsqueeze(3).to_broadcast(table), op=SUB
         )
 
         x_codes = [keep.tile([P, PASSES * P], U32, name="x_codes%d" % m, align_bytes=64) for m in range(TOK_TILES)]
@@ -142,7 +146,9 @@ def tile_transformerblock_pa_kernel(
         w_codes = {}
         w_scales = {}
         acc = {}
-        both = {}
+        sums = {}
+        products = {}
+        by_cos = {}
 
         def widen(u):
             c, g = divmod(u, PASSES)
@@ -164,8 +170,12 @@ def tile_transformerblock_pa_kernel(
             else:
                 rows = wide[u][:]
             packed[u] = grouped.tile([P, CHUNK * PACK], BF16, name="packed", align_bytes=64)
-            dst = packed[u][:].rearrange("p (c i t) -> p c t i", i=RUN, t=PACK)
-            src = rows.rearrange("p t (c i) -> p c t i", i=RUN)
+            if c in THREE_PRODUCTS:
+                dst = packed[u][:].rearrange("p (e c i t) -> p e c t i", e=2, i=RUN, t=PACK)
+                src = rows.rearrange("p t (c i e) -> p e c t i", i=RUN, e=2)
+            else:
+                dst = packed[u][:].rearrange("p (c i t) -> p c t i", i=RUN, t=PACK)
+                src = rows.rearrange("p t (c i) -> p c t i", i=RUN)
             if u >= FIRST_SCALAR_UNIT:
                 nc.scalar.copy(out=dst, in_=src)
             else:
@@ -178,40 +188,73 @@ def tile_transformerblock_pa_kernel(
                 out=w_codes[u][:].bitcast(FP8X4), scales=w_scales[u][:], in_=packed[u][:]
             )
 
+        def one_pass(out, m, u, cols, start, stop):
+            x_cols = slice(P * (u % PASSES), P * (u % PASSES + 1))
+            nc.tensor.matmul_mx(
+                out=out,
+                lhsT=x_codes[m][:, x_cols].bitcast(FP8X4),
+                lhsT_scale=x_scales[m][:, x_cols],
+                rhs=w_codes[u][:, cols].bitcast(FP8X4),
+                rhs_scale=w_scales[u][:, cols],
+                start=start,
+                stop=stop,
+            )
+
         def multiply(c, m, g):
             if g == 0:
                 acc[(c, m)] = psum.tile([P, CHUNK], F32, name="acc", tag="bank")
-            u = PASSES * c + g
-            cols = slice(P * g, P * (g + 1))
-            nc.tensor.matmul_mx(
-                out=acc[(c, m)][:],
-                lhsT=x_codes[m][:, cols].bitcast(FP8X4),
-                lhsT_scale=x_scales[m][:, cols],
-                rhs=w_codes[u][:].bitcast(FP8X4),
-                rhs_scale=w_scales[u][:],
-                start=(g == 0),
-                stop=(g == PASSES - 1),
-            )
+            one_pass(acc[(c, m)][:], m, PASSES * c + g, slice(0, CHUNK), g == 0, g == PASSES - 1)
 
-        def times_tables(b):
-            c, m = divmod(b, TOK_TILES)
-            both[b] = rope.tile([P, 2, CHUNK], F32, name="both")
-            shape = [P, 2, HEADS_PER_CHUNK, HEAD]
+        def add_pairs(c, j):
+            sums[(c, j)] = psum.tile([P, 2, HALF], F32, name="sums", tag="bank")
+            for i in range(2):
+                for n in range(2 * PASSES):
+                    g, e = divmod(n, 2)
+                    one_pass(
+                        sums[(c, j)][:, i, :], 2 * j + i, PASSES * c + g,
+                        slice(HALF * e, HALF * (e + 1)), n == 0, n == 2 * PASSES - 1,
+                    )
+
+        shape = [P, HEADS_PER_CHUNK, HEAD // 2, 2]
+        angles = "p (h i e) -> p h i e"
+
+        def four_products(c, m):
+            products[(c, m)] = rope.tile([P, 2, CHUNK], F32, name="products")
+            cos = cos_raw[:, m, :].unsqueeze(2).to_broadcast([P, HEAD // 2, 2])
+            for s, factor in ((0, cos), (1, signed_sin[:, m, :, :])):
+                nc.vector.tensor_tensor(
+                    out=products[(c, m)][:, s, :].rearrange(angles, i=HEAD // 2, e=2),
+                    in0=acc[(c, m)][:].rearrange(angles, i=HEAD // 2, e=2),
+                    in1=factor.unsqueeze(1).to_broadcast(shape),
+                    op=MULT,
+                )
+
+        def three_products(c, m):
+            products[(c, m)] = rope.tile([P, CHUNK], F32, name="products")
             nc.vector.tensor_tensor(
-                out=both[b][:].rearrange("p s (h d) -> p s h d", d=HEAD),
-                in0=acc[(c, m)][:].rearrange("p (h d) -> p h d", d=HEAD).unsqueeze(1).to_broadcast(shape),
-                in1=tables[:, m, :, :].unsqueeze(2).to_broadcast(shape),
+                out=products[(c, m)][:].rearrange(angles, i=HEAD // 2, e=2),
+                in0=acc[(c, m)][:].rearrange("p (e h i) -> p h i e", e=2, i=HEAD // 2),
+                in1=turn[:, m, :, :].unsqueeze(1).to_broadcast(shape),
+                op=MULT,
+            )
+            by_cos[(c, m)] = rope.tile([P, HALF], F32, name="by_cos")
+            nc.vector.tensor_tensor(
+                out=by_cos[(c, m)][:].rearrange("p (h i) -> p h i", i=HEAD // 2),
+                in0=sums[(c, m // 2)][:, m % 2, :].rearrange("p (h i) -> p h i", i=HEAD // 2),
+                in1=cos_raw[:, m, :].unsqueeze(1).to_broadcast(shape[0:3]),
                 op=MULT,
             )
 
-        def add_and_store(b, engine):
-            c, m = divmod(b, TOK_TILES)
+        def add_and_store(c, m, engine):
             res = result.tile([P, CHUNK], F32, name="res")
+            if c in THREE_PRODUCTS:
+                first = by_cos[(c, m)][:].unsqueeze(2).to_broadcast([P, HALF, 2])
+                second = products[(c, m)][:].rearrange("p (j e) -> p j e", e=2)
+            else:
+                first = products[(c, m)][:, 0, :].rearrange("p (j e) -> p j e", e=2)
+                second = products[(c, m)][:, 1, :].rearrange("p (j e) -> p j e", e=2)
             engine.tensor_tensor(
-                out=res[:].rearrange("p (j e) -> p j e", e=2),
-                in0=both[b][:, 0, :].rearrange("p (j e) -> p j e", e=2),
-                in1=both[b][:, 1, :].rearrange("p (j e) -> p j e", e=2)[:, :, ::-1],
-                op=ADD,
+                out=res[:].rearrange("p (j e) -> p j e", e=2), in0=first, in1=second[:, :, ::-1], op=ADD
             )
             rows = slice(P * m, P * (m + 1))
             if c == 0:
@@ -233,45 +276,77 @@ def tile_transformerblock_pa_kernel(
         for m in range(TOK_TILES):
             turn_x(m)
         widened = UNITS_BEFORE_X
-        passes_issued = 2 * PASSES
         left_to_vector = []
 
         def unit_at(i):
             return (i % 2) * PASSES + i // 2 if i < 2 * PASSES else i
+
+        pending = []
+        for c in range(CHUNKS):
+            pending = pending + [(c, g, m) for g in range(PASSES) for m in range(TOK_TILES)]
+            if c in THREE_PRODUCTS:
+                pending = pending + [(c, PASSES, j) for j in range(TOK_TILES // 2)]
+        quantised = set()
+        banks = []
+        emptied = set()
+
+        def ready(c, g, m):
+            if not all(PASSES * c + i in quantised for i in (range(PASSES) if g == PASSES else [g])):
+                return False
+            if g == 0 or g == PASSES:
+                return len(banks) < PSUM_BANKS or banks[len(banks) - PSUM_BANKS] in emptied
+            return (c, 0, m) in banks
+
+        def work_tensor():
+            left = []
+            blocked = False
+            for c, g, m in pending:
+                opens = g == 0 or g == PASSES
+                if (opens and blocked) or not ready(c, g, m):
+                    blocked = blocked or opens
+                    left.append((c, g, m))
+                    continue
+                if opens:
+                    banks.append((c, g, m))
+                if g == PASSES:
+                    add_pairs(c, m)
+                else:
+                    multiply(c, m, g)
+            return left
 
         interleave(unit_at(0))
         for u in range(UNITS):
             while widened < min(u + WIDEN_AHEAD, last_q):
                 widen(widened)
                 widened += 1
-            if u == HEAD_UNITS:
-                for m in range(TOK_TILES):
-                    quantise_x(m)
             if u + 1 < UNITS:
                 interleave(unit_at(u + 1))
             quantise(unit_at(u))
-            if u < HEAD_UNITS:
-                continue
-            if u <= UNITS - PASSES or u == UNITS - 1:
-                for b in left_to_vector:
-                    add_and_store(b, nc.vector)
-                left_to_vector = []
+            quantised.add(unit_at(u))
             if u == HEAD_UNITS:
-                for b in range(2 * TOK_TILES):
-                    for g in range(PASSES):
-                        multiply(b // TOK_TILES, b % TOK_TILES, g)
-            group = [TOK_TILES * c + m for c in ROPE_AFTER.get(u, ()) for m in range(TOK_TILES)]
-            for i, b in enumerate(group):
-                times_tables(b)
-                if 0 < i <= len(group) - VECTOR_ADDS:
-                    add_and_store(b - 1, nc.gpsimd)
-            left_to_vector = left_to_vector + group[len(group) - VECTOR_ADDS :]
-            if u == HEAD_UNITS:
+                for m in range(TOK_TILES):
+                    quantise_x(m)
+            for c, m in left_to_vector:
+                add_and_store(c, m, nc.vector)
+            left_to_vector = []
+            for c in ROPE_AFTER.get(u, ()):
+                group = [(c, m ^ 1 if c in THREE_PRODUCTS else m) for m in range(TOK_TILES)]
+                for i, (c, m) in enumerate(group):
+                    if c in THREE_PRODUCTS:
+                        three_products(c, m)
+                        emptied.add((c, PASSES, m // 2))
+                    else:
+                        four_products(c, m)
+                    emptied.add((c, 0, m))
+                    if 0 < i <= len(group) - VECTOR_ADDS:
+                        add_and_store(*group[i - 1], nc.gpsimd)
+                left_to_vector = group[len(group) - VECTOR_ADDS :]
+            if u == HEAD_UNITS + 2:
                 for g in range(PASSES):
                     nc.sync.dma_start(out=wv_raw[:, PACK * g : PACK * (g + 1), :], in_=wv_view[g])
-            while passes_issued <= u:
-                for m in range(TOK_TILES):
-                    multiply(passes_issued // PASSES, m, passes_issued % PASSES)
-                passes_issued += 1
+            if u >= HEAD_UNITS:
+                pending = work_tensor()
+        for c, m in left_to_vector:
+            add_and_store(c, m, nc.vector)
         for m in range(TOK_TILES):
             copy_and_store(m)

@@ -34,7 +34,14 @@ HEAD_UNITS = 7
 UNITS_BEFORE_X = 10
 FIRST_SCALAR_UNIT = 16
 WIDEN_AHEAD = 6
-ROPE_AFTER = {9: (0,), 12: (1,), 15: (2,), 19: (3,), 22: (4,)}
+ROPE_AFTER = {
+    9: (0, range(TOK_TILES)),
+    12: (1, range(TOK_TILES)),
+    15: (2, range(TOK_TILES)),
+    19: (3, range(TOK_TILES)),
+    UNITS - 2: (4, range(TOK_TILES // 2)),
+    UNITS - 1: (4, range(TOK_TILES // 2, TOK_TILES)),
+}
 VECTOR_ADDS = 2
 RUN = 8
 PSUM_BANKS = 8
@@ -264,10 +271,7 @@ def tile_transformerblock_pa_kernel(
 
         def copy_and_store(m):
             res = result.tile([P, CHUNK], F32, name="res")
-            if m % 2 == 0:
-                nc.scalar.copy(out=res[:], in_=acc[(CHUNKS - 1, m)][:])
-            else:
-                nc.vector.tensor_copy(out=res[:], in_=acc[(CHUNKS - 1, m)][:])
+            nc.scalar.copy(out=res[:], in_=acc[(CHUNKS - 1, m)][:])
             nc.sync.dma_start(out=v_out[P * m : P * (m + 1), :], in_=res[:])
 
         first_q, last_q = PASSES, PASSES * (Q_CHUNKS + 1)
@@ -329,8 +333,10 @@ def tile_transformerblock_pa_kernel(
             for c, m in left_to_vector:
                 add_and_store(c, m, nc.vector)
             left_to_vector = []
-            for c in ROPE_AFTER.get(u, ()):
-                group = [(c, m ^ 1 if c in THREE_PRODUCTS else m) for m in range(TOK_TILES)]
+            if u in ROPE_AFTER:
+                chunk, tiles = ROPE_AFTER[u]
+                group = [(chunk, m ^ 1 if chunk in THREE_PRODUCTS else m) for m in tiles]
+                by_vector = 1 if u == UNITS - 2 else VECTOR_ADDS
                 for i, (c, m) in enumerate(group):
                     if c in THREE_PRODUCTS:
                         three_products(c, m)
@@ -338,15 +344,15 @@ def tile_transformerblock_pa_kernel(
                     else:
                         four_products(c, m)
                     emptied.add((c, 0, m))
-                    if 0 < i <= len(group) - VECTOR_ADDS:
+                    if 0 < i <= len(group) - by_vector:
                         add_and_store(*group[i - 1], nc.gpsimd)
-                left_to_vector = group[len(group) - VECTOR_ADDS :]
+                left_to_vector = group[len(group) - by_vector :]
             if u == HEAD_UNITS + 2:
                 for g in range(PASSES):
                     nc.sync.dma_start(out=wv_raw[:, PACK * g : PACK * (g + 1), :], in_=wv_view[g])
             if u >= HEAD_UNITS:
                 pending = work_tensor()
-        for c, m in left_to_vector:
-            add_and_store(c, m, nc.vector)
         for m in range(TOK_TILES):
             copy_and_store(m)
+        for c, m in left_to_vector:
+            add_and_store(c, m, nc.vector)

@@ -32,17 +32,20 @@ HALF = CHUNK // 2
 THREE_PRODUCTS = (1, 3)
 HEAD_UNITS = 7
 UNITS_BEFORE_X = 10
-FIRST_SCALAR_UNIT = 16
-WIDEN_AHEAD = 6
+FIRST_SCALAR_UNIT = 13
+GPSIMD_UNIT = {9: 11, 12: 14, 15: 16, 17: 21}
+SHARED_UNIT = 19
+WIDEN_AHEAD = 4
+SCALAR_AHEAD = 2
 ROPE_AFTER = {
     9: (0, range(TOK_TILES)),
     12: (1, range(TOK_TILES)),
     15: (2, range(TOK_TILES)),
-    19: (3, range(TOK_TILES)),
-    UNITS - 2: (4, range(TOK_TILES // 2)),
-    UNITS - 1: (4, range(TOK_TILES // 2, TOK_TILES)),
+    17: (3, range(TOK_TILES)),
+    UNITS - 3: (4, range(1)),
+    UNITS - 2: (4, range(1, 2)),
+    UNITS - 1: (4, range(2, TOK_TILES)),
 }
-VECTOR_ADDS = 2
 RUN = 8
 PSUM_BANKS = 8
 
@@ -63,6 +66,8 @@ def tile_transformerblock_pa_kernel(
         keep = ctx.enter_context(tc.tile_pool(name="keep", bufs=1))
         planes = ctx.enter_context(tc.tile_pool(name="planes", bufs=7))
         grouped = ctx.enter_context(tc.tile_pool(name="grouped", bufs=4))
+        packed_by_vector = ctx.enter_context(tc.tile_pool(name="packed_by_vector", bufs=3))
+        packed_by_gpsimd = ctx.enter_context(tc.tile_pool(name="packed_by_gpsimd", bufs=2))
         quant = ctx.enter_context(tc.tile_pool(name="quant", bufs=12))
         rope = ctx.enter_context(tc.tile_pool(name="rope", bufs=4))
         result = ctx.enter_context(tc.tile_pool(name="result", bufs=8))
@@ -128,7 +133,7 @@ def tile_transformerblock_pa_kernel(
 
         def turn_x(m):
             words = x_raw[m][:].bitcast(F32)
-            x_grouped[m] = grouped.tile([P, PASSES * P * PACK], BF16, name="x_grouped", align_bytes=64)
+            x_grouped[m] = grouped.tile([P, PASSES * P * PACK], BF16, name="x_grouped", tag="grouped", align_bytes=64)
             x_words = x_grouped[m][:].bitcast(F32).rearrange("p (g r u) -> p g r u", g=PASSES, u=2)
             for half in range(2):
                 turned = psum.tile([P, 2, 2, P], F32, name="turned", tag="bank")
@@ -150,6 +155,7 @@ def tile_transformerblock_pa_kernel(
 
         wide = {}
         packed = {}
+        other_half = {}
         w_codes = {}
         w_scales = {}
         acc = {}
@@ -168,25 +174,43 @@ def tile_transformerblock_pa_kernel(
                     scale=scales[:, g, t : t + 1],
                 )
 
-        def interleave(u):
+        def rows_of(u):
             c, g = divmod(u, PASSES)
             if c == 0:
-                rows = wk_raw[:, PACK * g : PACK * (g + 1), :]
-            elif c == CHUNKS - 1:
-                rows = wv_raw[:, PACK * g : PACK * (g + 1), :]
-            else:
-                rows = wide[u][:]
-            packed[u] = grouped.tile([P, CHUNK * PACK], BF16, name="packed", align_bytes=64)
-            if c in THREE_PRODUCTS:
+                return wk_raw[:, PACK * g : PACK * (g + 1), :]
+            if c == CHUNKS - 1:
+                return wv_raw[:, PACK * g : PACK * (g + 1), :]
+            return wide[u][:]
+
+        def interleave(u):
+            pool = grouped if u >= FIRST_SCALAR_UNIT else packed_by_vector
+            packed[u] = pool.tile([P, CHUNK * PACK], BF16, name="packed", tag="grouped", align_bytes=64)
+            if u // PASSES in THREE_PRODUCTS:
                 dst = packed[u][:].rearrange("p (e c i t) -> p e c t i", e=2, i=RUN, t=PACK)
-                src = rows.rearrange("p t (c i e) -> p e c t i", i=RUN, e=2)
+                src = rows_of(u).rearrange("p t (c i e) -> p e c t i", i=RUN, e=2)
             else:
                 dst = packed[u][:].rearrange("p (c i t) -> p c t i", i=RUN, t=PACK)
-                src = rows.rearrange("p t (c i) -> p c t i", i=RUN)
-            if u >= FIRST_SCALAR_UNIT:
+                src = rows_of(u).rearrange("p t (c i) -> p c t i", i=RUN)
+            if u == SHARED_UNIT:
+                half = CHUNK // RUN // 2
+                nc.scalar.copy(out=dst[:, 0:half], in_=src[:, 0:half])
+                other_half[u] = (dst[:, half:], src[:, half:])
+            elif u >= FIRST_SCALAR_UNIT:
                 nc.scalar.copy(out=dst, in_=src)
             else:
                 nc.vector.tensor_copy(out=dst, in_=src)
+
+        def interleave_on_gpsimd(u):
+            packed[u] = packed_by_gpsimd.tile([P, CHUNK * PACK], BF16, name="packed", tag="grouped", align_bytes=64)
+            one = keep.tile([P, 1], F32, name="one%d" % u)
+            nc.vector.memset(one[:], 1.0)
+            if u // PASSES in THREE_PRODUCTS:
+                dst = packed[u][:].rearrange("p (e j t) -> p e j t", e=2, t=PACK)
+                src = rows_of(u).rearrange("p t (j e) -> p e j t", e=2)
+            else:
+                dst = packed[u][:].rearrange("p (n t) -> p n t", t=PACK)
+                src = rows_of(u).rearrange("p t n -> p n t")
+            nc.gpsimd.tensor_scalar(out=dst, in0=src, scalar1=one[:], scalar2=0.0, op0=MULT, op1=ADD)
 
         def quantise(u):
             w_codes[u] = quant.tile([P, CHUNK], U32, name="w_codes", align_bytes=64)
@@ -318,13 +342,24 @@ def tile_transformerblock_pa_kernel(
                     multiply(c, m, g)
             return left
 
-        interleave(unit_at(0))
+        by_gpsimd = [GPSIMD_UNIT[u] for u in GPSIMD_UNIT]
+        vector_units = [u for u in map(unit_at, range(FIRST_SCALAR_UNIT)) if u not in by_gpsimd]
+        scalar_units = [u for u in range(FIRST_SCALAR_UNIT, UNITS) if u not in by_gpsimd]
+
+        interleave(vector_units[0])
         for u in range(UNITS):
             while widened < min(u + WIDEN_AHEAD, last_q):
                 widen(widened)
                 widened += 1
-            if u + 1 < UNITS:
-                interleave(unit_at(u + 1))
+            for w in scalar_units:
+                if w <= u + SCALAR_AHEAD and w not in packed:
+                    interleave(w)
+            following = [w for w in vector_units if w not in packed]
+            if following and unit_at(u) in packed:
+                interleave(following[0])
+            if u + 1 == SHARED_UNIT:
+                dst, src = other_half[SHARED_UNIT]
+                nc.vector.tensor_copy(out=dst, in_=src)
             quantise(unit_at(u))
             quantised.add(unit_at(u))
             if u == HEAD_UNITS:
@@ -336,7 +371,9 @@ def tile_transformerblock_pa_kernel(
             if u in ROPE_AFTER:
                 chunk, tiles = ROPE_AFTER[u]
                 group = [(chunk, m ^ 1 if chunk in THREE_PRODUCTS else m) for m in tiles]
-                by_vector = 1 if u == UNITS - 2 else VECTOR_ADDS
+                by_vector = len(tiles) - (1 if len(tiles) == TOK_TILES and chunk not in THREE_PRODUCTS else 0)
+                if u in GPSIMD_UNIT:
+                    interleave_on_gpsimd(GPSIMD_UNIT[u])
                 for i, (c, m) in enumerate(group):
                     if c in THREE_PRODUCTS:
                         three_products(c, m)

from contextlib import ExitStack

import concourse.mybir as mybir
from concourse.masks import make_identity

SEQ, DIM, HEAD = 512, 2048, 128
N_Q, N_K, N_V = 2048, 512, 512
FLOPS = 2 * SEQ * DIM * (N_Q + N_K + N_V)

F32 = mybir.dt.float32
BF16 = mybir.dt.bfloat16
U32 = mybir.dt.uint32
U8 = mybir.dt.uint8
E4M3 = mybir.dt.float8_e4m3fn
FP8X4 = mybir.dt.float8_e4m3fn_x4
MULT = mybir.AluOpType.mult
ADD = mybir.AluOpType.add
SUB = mybir.AluOpType.subtract
COPY = mybir.ActivationFunctionType.Copy

P = 128
PACK = 4
PASSES = DIM // (P * PACK)
TOK_TILES = SEQ // P
CHUNK = 512
HEADS_PER_CHUNK = CHUNK // HEAD
Q_CHUNKS = N_Q // CHUNK
CHUNKS = Q_CHUNKS + 2
UNITS = CHUNKS * PASSES
HALF = CHUNK // 2

THREE_PRODUCTS = (1, 3)
HEAD_UNITS = 7
UNITS_BEFORE_X = 10
FIRST_SCALAR_UNIT = 13
GPSIMD_UNIT = {9: 11, 12: 14, 15: 16, 17: 21}
SHARED_UNIT = 19
WIDEN_AHEAD = 4
SCALAR_AHEAD = 2
ROPE_AFTER = {
    9: (0, range(TOK_TILES)),
    12: (1, range(TOK_TILES)),
    15: (2, range(TOK_TILES)),
    17: (3, range(TOK_TILES)),
    UNITS - 3: (4, range(1)),
    UNITS - 2: (4, range(1, 2)),
    UNITS - 1: (4, range(2, TOK_TILES)),
}
RUN = 8
PSUM_BANKS = 8


def tile_transformerblock_pa_kernel(
    tc, x, freqs_cos, freqs_sin, wq_bytes, wq_scale, wk, wv, out_0, out_1, out_2
):
    nc = tc.nc
    x_rows = x.rearrange("b s d -> (b s) d")
    wq_view = wq_bytes.rearrange("(g p t) n -> g p t n", p=P, t=PACK)
    wk_view = wk.rearrange("(g p t) n -> g p t n", p=P, t=PACK)
    wv_view = wv.rearrange("(g p t) n -> g p t n", p=P, t=PACK)
    q_out = out_0.rearrange("b s h d -> (b s) (h d)")
    k_out = out_1.rearrange("b s h d -> (b s) (h d)")
    v_out = out_2.rearrange("b s h d -> (b s) (h d)")

    with ExitStack() as ctx:
        keep = ctx.enter_context(tc.tile_pool(name="keep", bufs=1))
        planes = ctx.enter_context(tc.tile_pool(name="planes", bufs=7))
        grouped = ctx.enter_context(tc.tile_pool(name="grouped", bufs=4))
        packed_by_vector = ctx.enter_context(tc.tile_pool(name="packed_by_vector", bufs=3))
        packed_by_gpsimd = ctx.enter_context(tc.tile_pool(name="packed_by_gpsimd", bufs=2))
        quant = ctx.enter_context(tc.tile_pool(name="quant", bufs=12))
        rope = ctx.enter_context(tc.tile_pool(name="rope", bufs=4))
        result = ctx.enter_context(tc.tile_pool(name="result", bufs=8))
        psum = ctx.enter_context(tc.psum_pool(name="psum", bufs=PSUM_BANKS))
        ctx.enter_context(tc.manual_schedule())

        scales = keep.tile([P, PASSES, PACK], F32, name="scales")
        wq_codes = [keep.tile([P, PASSES * PACK, CHUNK], U8, name="wq_codes%d" % j) for j in range(Q_CHUNKS)]
        x_raw = [keep.tile([P, DIM], BF16, name="x_raw%d" % m) for m in range(TOK_TILES)]
        wk_raw = keep.tile([P, PASSES * PACK, CHUNK], BF16, name="wk_raw")
        wv_raw = keep.tile([P, PASSES * PACK, CHUNK], BF16, name="wv_raw")
        cos_raw = keep.tile([P, TOK_TILES, HEAD // 2], BF16, name="cos_raw")
        sin_raw = keep.tile([P, TOK_TILES, HEAD // 2], BF16, name="sin_raw")

        def load_wq(j, g):
            nc.sync.dma_start(
                out=wq_codes[j][:, PACK * g : PACK * (g + 1), :],
                in_=wq_view[g][:, :, CHUNK * j : CHUNK * (j + 1)],
            )

        nc.sync.dma_start(
            out=scales[:], in_=wq_scale.rearrange("(g p t) o -> p g (t o)", p=P, t=PACK)
        )
        for g in range(PASSES):
            load_wq(0, g)
            if g == 0:
                nc.sync.dma_start(out=cos_raw[:], in_=freqs_cos.rearrange("(m p) i -> p m i", p=P))
                nc.sync.dma_start(out=sin_raw[:], in_=freqs_sin.rearrange("(m p) i -> p m i", p=P))
            nc.sync.dma_start(out=wk_raw[:, PACK * g : PACK * (g + 1), :], in_=wk_view[g])
        for u in range(2 * PASSES, UNITS_BEFORE_X):
            load_wq(u // PASSES - 1, u % PASSES)
        for m in range(TOK_TILES):
            nc.sync.dma_start(out=x_raw[m][:], in_=x_rows[P * m : P * (m + 1), :])
        for u in range(UNITS_BEFORE_X, PASSES * (Q_CHUNKS + 1)):
            load_wq(u // PASSES - 1, u % PASSES)

        zero = keep.tile([P, 1], F32, name="zero")
        warm = keep.tile([P, 1], F32, name="warm")
        nc.vector.memset(zero[:], 0.0)
        nc.scalar.activation(out=warm[:], in_=zero[:], func=COPY)
        ident = keep.tile([P, P], F32, name="ident")
        make_identity(nc, ident[:])

        sign = keep.tile([P, 2], F32, name="sign")
        nc.vector.memset(sign[:, 0:1], 1.0)
        nc.vector.memset(sign[:, 1:2], -1.0)
        signed_sin = keep.tile([P, TOK_TILES, HEAD // 2, 2], F32, name="signed_sin")
        turn = keep.tile([P, TOK_TILES, HEAD // 2, 2], F32, name="turn")
        table = [P, TOK_TILES, HEAD // 2, 2]
        nc.vector.tensor_tensor(
            out=signed_sin[:],
            in0=sin_raw[:].unsqueeze(3).to_broadcast(table),
            in1=sign[:].unsqueeze(1).unsqueeze(1).to_broadcast(table),
            op=MULT,
        )
        nc.vector.tensor_tensor(
            out=turn[:], in0=signed_sin[:], in1=cos_raw[:].unsqueeze(3).to_broadcast(table), op=SUB
        )

        x_codes = [keep.tile([P, PASSES * P], U32, name="x_codes%d" % m, align_bytes=64) for m in range(TOK_TILES)]
        x_scales = [keep.tile([P, PASSES * P], U8, name="x_scales%d" % m, align_bytes=64) for m in range(TOK_TILES)]
        x_grouped = {}

        def turn_x(m):
            words = x_raw[m][:].bitcast(F32)
            x_grouped[m] = grouped.tile([P, PASSES * P * PACK], BF16, name="x_grouped", tag="grouped", align_bytes=64)
            x_words = x_grouped[m][:].bitcast(F32).rearrange("p (g r u) -> p g r u", g=PASSES, u=2)
            for half in range(2):
                turned = psum.tile([P, 2, 2, P], F32, name="turned", tag="bank")
                for gg in range(2):
                    g = 2 * half + gg
                    for u in range(2):
                        nc.tensor.transpose(
                            turned[:, gg, u, :], words[:, 256 * g + u : 256 * (g + 1) : 2], ident[:]
                        )
                nc.scalar.copy(
                    out=x_words[:, 2 * half : 2 * half + 2, :, :],
                    in_=turned[:].rearrange("p g u r -> p g r u"),
                )

        def quantise_x(m):
            nc.vector.quantize_mx(
                out=x_codes[m][:].bitcast(FP8X4), scales=x_scales[m][:], in_=x_grouped[m][:]
            )

        wide = {}
        packed = {}
        other_half = {}
        w_codes = {}
        w_scales = {}
        acc = {}
        sums = {}
        products = {}
        by_cos = {}

        def widen(u):
            c, g = divmod(u, PASSES)
            wide[u] = planes.tile([P, PACK, CHUNK], BF16, name="wide")
            for t in range(PACK):
                nc.scalar.activation(
                    out=wide[u][:, t, :],
                    in_=wq_codes[c - 1][:, PACK * g + t, :].bitcast(E4M3),
                    func=COPY,
                    scale=scales[:, g, t : t + 1],
                )

        def rows_of(u):
            c, g = divmod(u, PASSES)
            if c == 0:
                return wk_raw[:, PACK * g : PACK * (g + 1), :]
            if c == CHUNKS - 1:
                return wv_raw[:, PACK * g : PACK * (g + 1), :]
            return wide[u][:]

        def interleave(u):
            pool = grouped if u >= FIRST_SCALAR_UNIT else packed_by_vector
            packed[u] = pool.tile([P, CHUNK * PACK], BF16, name="packed", tag="grouped", align_bytes=64)
            if u // PASSES in THREE_PRODUCTS:
                dst = packed[u][:].rearrange("p (e c i t) -> p e c t i", e=2, i=RUN, t=PACK)
                src = rows_of(u).rearrange("p t (c i e) -> p e c t i", i=RUN, e=2)
            else:
                dst = packed[u][:].rearrange("p (c i t) -> p c t i", i=RUN, t=PACK)
                src = rows_of(u).rearrange("p t (c i) -> p c t i", i=RUN)
            if u == SHARED_UNIT:
                half = CHUNK // RUN // 2
                nc.scalar.copy(out=dst[:, 0:half], in_=src[:, 0:half])
                other_half[u] = (dst[:, half:], src[:, half:])
            elif u >= FIRST_SCALAR_UNIT:
                nc.scalar.copy(out=dst, in_=src)
            else:
                nc.vector.tensor_copy(out=dst, in_=src)

        def interleave_on_gpsimd(u):
            packed[u] = packed_by_gpsimd.tile([P, CHUNK * PACK], BF16, name="packed", tag="grouped", align_bytes=64)
            one = keep.tile([P, 1], F32, name="one%d" % u)
            nc.vector.memset(one[:], 1.0)
            if u // PASSES in THREE_PRODUCTS:
                dst = packed[u][:].rearrange("p (e j t) -> p e j t", e=2, t=PACK)
                src = rows_of(u).rearrange("p t (j e) -> p e j t", e=2)
            else:
                dst = packed[u][:].rearrange("p (n t) -> p n t", t=PACK)
                src = rows_of(u).rearrange("p t n -> p n t")
            nc.gpsimd.tensor_scalar(out=dst, in0=src, scalar1=one[:], scalar2=0.0, op0=MULT, op1=ADD)

        def quantise(u):
            w_codes[u] = quant.tile([P, CHUNK], U32, name="w_codes", align_bytes=64)
            w_scales[u] = quant.tile([P, CHUNK], U8, name="w_scales", align_bytes=64)
            nc.vector.quantize_mx(
                out=w_codes[u][:].bitcast(FP8X4), scales=w_scales[u][:], in_=packed[u][:]
            )

        def one_pass(out, m, u, cols, start, stop):
            x_cols = slice(P * (u % PASSES), P * (u % PASSES + 1))
            nc.tensor.matmul_mx(
                out=out,
                lhsT=x_codes[m][:, x_cols].bitcast(FP8X4),
                lhsT_scale=x_scales[m][:, x_cols],
                rhs=w_codes[u][:, cols].bitcast(FP8X4),
                rhs_scale=w_scales[u][:, cols],
                start=start,
                stop=stop,
            )

        def multiply(c, m, g):
            if g == 0:
                acc[(c, m)] = psum.tile([P, CHUNK], F32, name="acc", tag="bank")
            one_pass(acc[(c, m)][:], m, PASSES * c + g, slice(0, CHUNK), g == 0, g == PASSES - 1)

        def add_pairs(c, j):
            sums[(c, j)] = psum.tile([P, 2, HALF], F32, name="sums", tag="bank")
            for i in range(2):
                for n in range(2 * PASSES):
                    g, e = divmod(n, 2)
                    one_pass(
                        sums[(c, j)][:, i, :], 2 * j + i, PASSES * c + g,
                        slice(HALF * e, HALF * (e + 1)), n == 0, n == 2 * PASSES - 1,
                    )

        shape = [P, HEADS_PER_CHUNK, HEAD // 2, 2]
        angles = "p (h i e) -> p h i e"

        def four_products(c, m):
            products[(c, m)] = rope.tile([P, 2, CHUNK], F32, name="products")
            cos = cos_raw[:, m, :].unsqueeze(2).to_broadcast([P, HEAD // 2, 2])
            for s, factor in ((0, cos), (1, signed_sin[:, m, :, :])):
                nc.vector.tensor_tensor(
                    out=products[(c, m)][:, s, :].rearrange(angles, i=HEAD // 2, e=2),
                    in0=acc[(c, m)][:].rearrange(angles, i=HEAD // 2, e=2),
                    in1=factor.unsqueeze(1).to_broadcast(shape),
                    op=MULT,
                )

        def three_products(c, m):
            products[(c, m)] = rope.tile([P, CHUNK], F32, name="products")
            nc.vector.tensor_tensor(
                out=products[(c, m)][:].rearrange(angles, i=HEAD // 2, e=2),
                in0=acc[(c, m)][:].rearrange("p (e h i) -> p h i e", e=2, i=HEAD // 2),
                in1=turn[:, m, :, :].unsqueeze(1).to_broadcast(shape),
                op=MULT,
            )
            by_cos[(c, m)] = rope.tile([P, HALF], F32, name="by_cos")
            nc.vector.tensor_tensor(
                out=by_cos[(c, m)][:].rearrange("p (h i) -> p h i", i=HEAD // 2),
                in0=sums[(c, m // 2)][:, m % 2, :].rearrange("p (h i) -> p h i", i=HEAD // 2),
                in1=cos_raw[:, m, :].unsqueeze(1).to_broadcast(shape[0:3]),
                op=MULT,
            )

        def add_and_store(c, m, engine):
            res = result.tile([P, CHUNK], F32, name="res")
            if c in THREE_PRODUCTS:
                first = by_cos[(c, m)][:].unsqueeze(2).to_broadcast([P, HALF, 2])
                second = products[(c, m)][:].rearrange("p (j e) -> p j e", e=2)
            else:
                first = products[(c, m)][:, 0, :].rearrange("p (j e) -> p j e", e=2)
                second = products[(c, m)][:, 1, :].rearrange("p (j e) -> p j e", e=2)
            engine.tensor_tensor(
                out=res[:].rearrange("p (j e) -> p j e", e=2), in0=first, in1=second[:, :, ::-1], op=ADD
            )
            rows = slice(P * m, P * (m + 1))
            if c == 0:
                nc.sync.dma_start(out=k_out[rows, :], in_=res[:])
            else:
                nc.sync.dma_start(out=q_out[rows, CHUNK * (c - 1) : CHUNK * c], in_=res[:])

        def copy_and_store(m):
            res = result.tile([P, CHUNK], F32, name="res")
            nc.scalar.copy(out=res[:], in_=acc[(CHUNKS - 1, m)][:])
            nc.sync.dma_start(out=v_out[P * m : P * (m + 1), :], in_=res[:])

        first_q, last_q = PASSES, PASSES * (Q_CHUNKS + 1)
        for u in range(first_q, UNITS_BEFORE_X):
            widen(u)
        for m in range(TOK_TILES):
            turn_x(m)
        widened = UNITS_BEFORE_X
        left_to_vector = []

        def unit_at(i):
            return (i % 2) * PASSES + i // 2 if i < 2 * PASSES else i

        pending = []
        for c in range(CHUNKS):
            pending = pending + [(c, g, m) for g in range(PASSES) for m in range(TOK_TILES)]
            if c in THREE_PRODUCTS:
                pending = pending + [(c, PASSES, j) for j in range(TOK_TILES // 2)]
        quantised = set()
        banks = []
        emptied = set()

        def ready(c, g, m):
            if not all(PASSES * c + i in quantised for i in (range(PASSES) if g == PASSES else [g])):
                return False
            if g == 0 or g == PASSES:
                return len(banks) < PSUM_BANKS or banks[len(banks) - PSUM_BANKS] in emptied
            return (c, 0, m) in banks

        def work_tensor():
            left = []
            blocked = False
            for c, g, m in pending:
                opens = g == 0 or g == PASSES
                if (opens and blocked) or not ready(c, g, m):
                    blocked = blocked or opens
                    left.append((c, g, m))
                    continue
                if opens:
                    banks.append((c, g, m))
                if g == PASSES:
                    add_pairs(c, m)
                else:
                    multiply(c, m, g)
            return left

        by_gpsimd = [GPSIMD_UNIT[u] for u in GPSIMD_UNIT]
        vector_units = [u for u in map(unit_at, range(FIRST_SCALAR_UNIT)) if u not in by_gpsimd]
        scalar_units = [u for u in range(FIRST_SCALAR_UNIT, UNITS) if u not in by_gpsimd]

        interleave(vector_units[0])
        for u in range(UNITS):
            while widened < min(u + WIDEN_AHEAD, last_q):
                widen(widened)
                widened += 1
            for w in scalar_units:
                if w <= u + SCALAR_AHEAD and w not in packed:
                    interleave(w)
            following = [w for w in vector_units if w not in packed]
            if following and unit_at(u) in packed:
                interleave(following[0])
            if u + 1 == SHARED_UNIT:
                dst, src = other_half[SHARED_UNIT]
                nc.vector.tensor_copy(out=dst, in_=src)
            quantise(unit_at(u))
            quantised.add(unit_at(u))
            if u == HEAD_UNITS:
                for m in range(TOK_TILES):
                    quantise_x(m)
            for c, m in left_to_vector:
                add_and_store(c, m, nc.vector)
            left_to_vector = []
            if u in ROPE_AFTER:
                chunk, tiles = ROPE_AFTER[u]
                group = [(chunk, m ^ 1 if chunk in THREE_PRODUCTS else m) for m in tiles]
                by_vector = len(tiles) - (1 if len(tiles) == TOK_TILES and chunk not in THREE_PRODUCTS else 0)
                if u in GPSIMD_UNIT:
                    interleave_on_gpsimd(GPSIMD_UNIT[u])
                for i, (c, m) in enumerate(group):
                    if c in THREE_PRODUCTS:
                        three_products(c, m)
                        emptied.add((c, PASSES, m // 2))
                    else:
                        four_products(c, m)
                    emptied.add((c, 0, m))
                    if 0 < i <= len(group) - by_vector:
                        add_and_store(*group[i - 1], nc.gpsimd)
                left_to_vector = group[len(group) - by_vector :]
            if u == HEAD_UNITS + 2:
                for g in range(PASSES):
                    nc.sync.dma_start(out=wv_raw[:, PACK * g : PACK * (g + 1), :], in_=wv_view[g])
            if u >= HEAD_UNITS:
                pending = work_tensor()
        for m in range(TOK_TILES):
            copy_and_store(m)
        for c, m in left_to_vector:
            add_and_store(c, m, nc.vector)
